import numpy as np
import ml_dtypes


def mxq(x, axis, fmt="e4m3"):
    dtype, down = {"e4m3": (ml_dtypes.float8_e4m3fn, 7), "e5m2": (ml_dtypes.float8_e5m2, 14)}[fmt]
    v = np.moveaxis(np.asarray(x, np.float32).astype(ml_dtypes.bfloat16).astype(np.float64), axis, -1)
    blocks = v.reshape(v.shape[:-1] + (-1, 32))
    amax = np.abs(blocks).max(-1, keepdims=True)
    byte = np.maximum(np.where(amax > 0, np.frexp(amax)[1] - 1 + 127, 0) - down, 1)
    scale = np.exp2(byte - 127.0)
    codes = (blocks / scale).astype(np.float32).astype(dtype).astype(np.float64)
    return np.moveaxis((codes * scale).reshape(v.shape), -1, axis)


WIDE = False


def mx_kscale(k):
    if not WIDE:
        return np.ones(k)
    levels = np.array([10, -10, 5, -5, 0])
    a = np.random.permutation(np.resize(levels, k // 512 * 4)).reshape(k // 512, 4)
    idx = np.arange(k)
    return np.exp2(a[idx // 512, idx % 128 // 32])


BF16 = ml_dtypes.bfloat16


def bf(x):
    return np.asarray(x, np.float32).astype(BF16)


def f64(x):
    return np.asarray(x).astype(np.float64)


B, V, H, CD = 128, 16384, 512, 1


def sigmoid(x):
    return 0.5 * (1.0 + np.tanh(0.5 * x))


def setup_inputs():
    s = mx_kscale(V)
    s = s / s.min()
    return {"v": bf(np.random.uniform(size=(B, V)) * s),
            "w": bf(np.random.standard_normal((V, H)) * 1.5 / np.sqrt(V) / s[:, None]),
            "vb": bf(np.random.standard_normal(V) * 0.5 / s),
            "hb": bf(np.random.standard_normal(H) * 0.3)}


def reference(v, w, vb, hb):
    v, w = f64(v), f64(w)
    h_p = sigmoid(f64(hb) + (mxq(v, 1, "e4m3") @ mxq(w, 0, "e4m3")))
    v_prediction = sigmoid(f64(vb) + (mxq(h_p, 1, "e4m3") @ mxq(w.T, 0, "e4m3")))
    return h_p, v_prediction

@@ -1,0 +1,224 @@
+from contextlib import ExitStack
+
+import concourse.mybir as mybir
+from concourse.masks import make_identity
+
+F32 = mybir.dt.float32
+BF16 = mybir.dt.bfloat16
+U32 = mybir.dt.uint32
+U8 = mybir.dt.uint8
+FP8X4 = mybir.dt.float8_e4m3fn_x4
+ADD = mybir.AluOpType.add
+SIGMOID = mybir.ActivationFunctionType.Sigmoid
+
+P = 128
+PACK = 4
+K_PASS = P * PACK
+BANK = 512
+
+BATCH = 128
+VISIBLE = 16384
+HIDDEN = 512
+
+PASSES = 2
+STEP_ROWS = PASSES * K_PASS
+STEPS = VISIBLE // STEP_ROWS
+VECTOR_COLS = 352
+RUN = 4
+BIAS_PARTS = 4
+OUT_COLS = 1024
+
+FLOPS = 2 * 2 * BATCH * VISIBLE * HIDDEN
+
+
+def tile_rbm_pa_k_kernel(tc, v, w, vb, hb, out_0, out_1):
+    nc = tc.nc
+    w_steps = w.rearrange("(s g p r) h -> s p g (r h)", g=PASSES, p=P, r=PACK)
+    vb_rows = vb.partition_broadcast(P)
+    hb_rows = hb.partition_broadcast(P)
+
+    with ExitStack() as whole:
+        whole.enter_context(tc.manual_schedule())
+        keep = whole.enter_context(tc.tile_pool(name="keep", bufs=1))
+        sum_bank = whole.enter_context(tc.psum_pool(name="sum_bank", bufs=1))
+        banks = whole.enter_context(tc.psum_pool(name="banks", bufs=7))
+
+        ident_f32 = keep.tile([P, P], F32)
+        make_identity(nc, ident_f32[:])
+        ident_bf16 = keep.tile([P, P], BF16)
+        make_identity(nc, ident_bf16[:])
+
+        warm = keep.tile([P, 2], F32)
+        nc.vector.memset(warm[:], 0.0)
+        nc.scalar.activation(out=warm[:, 1:2], in_=warm[:, 0:1], func=SIGMOID)
+
+        down_codes = keep.tile([P, VISIBLE], U32, align_bytes=64)
+        down_scales = keep.tile([P, VISIBLE], U8, align_bytes=64)
+        vb_all = keep.tile([P, VISIBLE], BF16)
+        hb_all = keep.tile([P, HIDDEN], BF16)
+        hidden_sum = sum_bank.tile([BATCH, HIDDEN], F32)
+
+        with ExitStack() as up:
+            w_pool = up.enter_context(tc.tile_pool(name="w_pool", bufs=5))
+            v_pool = up.enter_context(tc.tile_pool(name="v_pool", bufs=4))
+            grouped = up.enter_context(tc.tile_pool(name="grouped", bufs=2))
+            operands = up.enter_context(tc.tile_pool(name="operands", bufs=3))
+
+            def load(s):
+                w_rows = w_pool.tile([P, PASSES * PACK * HIDDEN], BF16)
+                for g in range(PASSES):
+                    here = slice(g * PACK * HIDDEN, (g + 1) * PACK * HIDDEN)
+                    nc.sync.dma_start(out=w_rows[:, here], in_=w_steps[s, :, g, :])
+                v_cols = v_pool.tile([BATCH, STEP_ROWS], BF16)
+                nc.sync.dma_start(out=v_cols[:], in_=v[:, s * STEP_ROWS : (s + 1) * STEP_ROWS])
+                if s % BIAS_PARTS == 1:
+                    part = VISIBLE // BIAS_PARTS
+                    cols = slice((s // BIAS_PARTS) * part, (s // BIAS_PARTS + 1) * part)
+                    nc.sync.dma_start(out=vb_all[:, cols], in_=vb_rows[:, cols])
+                if s == STEPS // 2:
+                    nc.sync.dma_start(out=hb_all[:], in_=hb_rows)
+                return w_rows, v_cols
+
+            def lay_rows_side_by_side(w_rows):
+                up_grouped = grouped.tile([P, PASSES * HIDDEN * PACK], BF16, align_bytes=64)
+                src = w_rows[:].rearrange("p (g r c i) -> p g c r i", g=PASSES, r=PACK, i=RUN)
+                dst = up_grouped[:].rearrange("p (g c i r) -> p g c r i", g=PASSES, r=PACK, i=RUN)
+                split = VECTOR_COLS // RUN
+                for g in range(PASSES):
+                    nc.vector.tensor_copy(out=dst[:, g, :split], in_=src[:, g, :split])
+                    nc.scalar.copy(out=dst[:, g, split:], in_=src[:, g, split:])
+                return up_grouped
+
+            def transpose(w_rows, v_cols):
+                v_words = v_cols[:].bitcast(F32).rearrange("b (g q u) -> b g u q", g=PASSES, u=2)
+                v_bank = banks.tile([P, PASSES * 2, BATCH], F32, tag="bank")
+                for g in range(PASSES):
+                    for u in range(2):
+                        nc.tensor.transpose(v_bank[:, 2 * g + u, :], v_words[:, g, u, :], ident_f32[:])
+                w_words = w_rows[:].bitcast(F32).rearrange(
+                    "q (g a r u i) -> q g a r u i", g=PASSES, a=2, r=2, u=2
+                )
+                w_banks = []
+                for g in range(PASSES):
+                    for a in range(2):
+                        w_bank = banks.tile([P, 4, P], F32, tag="bank", name="w_bank")
+                        for r in range(2):
+                            for u in range(2):
+                                nc.tensor.transpose(
+                                    w_bank[:, 2 * r + u, :], w_words[:, g, a, r, u, :], ident_f32[:]
+                                )
+                        w_banks.append(w_bank)
+                return v_bank, w_banks
+
+            def empty_banks(v_bank, w_banks):
+                v_grouped = grouped.tile([P, PASSES * BATCH * PACK], BF16, align_bytes=64)
+                nc.scalar.copy(
+                    out=v_grouped[:].bitcast(F32).rearrange("p (g b u) -> p g b u", g=PASSES, u=2),
+                    in_=v_bank[:].rearrange("p (g u) b -> p g b u", u=2),
+                )
+                down_grouped = grouped.tile([P, STEP_ROWS * PACK], BF16, align_bytes=64)
+                dst = down_grouped[:].bitcast(F32).rearrange(
+                    "p (n r q u) -> p n r q u", n=len(w_banks), r=2, u=2
+                )
+                for n, w_bank in enumerate(w_banks):
+                    nc.scalar.copy(
+                        out=dst[:, n], in_=w_bank[:].rearrange("p (r u) q -> p r q u", u=2)
+                    )
+                return v_grouped, down_grouped
+
+            def quantise_up(up_grouped, v_grouped):
+                w_codes = operands.tile([P, PASSES * HIDDEN], U32, align_bytes=64)
+                w_scales = operands.tile([P, PASSES * HIDDEN], U8, align_bytes=64)
+                nc.vector.quantize_mx(
+                    out=w_codes[:].bitcast(FP8X4), scales=w_scales[:], in_=up_grouped[:]
+                )
+                v_codes = operands.tile([P, PASSES * BATCH], U32, align_bytes=64)
+                v_scales = operands.tile([P, PASSES * BATCH], U8, align_bytes=64)
+                nc.vector.quantize_mx(
+                    out=v_codes[:].bitcast(FP8X4), scales=v_scales[:], in_=v_grouped[:]
+                )
+                return w_codes, w_scales, v_codes, v_scales
+
+            def first_matmul(s, w_codes, w_scales, v_codes, v_scales):
+                for g in range(PASSES):
+                    b_cols = slice(g * BATCH, (g + 1) * BATCH)
+                    h_cols = slice(g * HIDDEN, (g + 1) * HIDDEN)
+                    nc.tensor.matmul_mx(
+                        out=hidden_sum[:],
+                        lhsT=v_codes[:, b_cols].bitcast(FP8X4),
+                        lhsT_scale=v_scales[:, b_cols],
+                        rhs=w_codes[:, h_cols].bitcast(FP8X4),
+                        rhs_scale=w_scales[:, h_cols],
+                        start=(s == 0 and g == 0),
+                        stop=(s == STEPS - 1 and g == PASSES - 1),
+                    )
+
+            def quantise_down(s, down_grouped):
+                cols = slice(s * STEP_ROWS, (s + 1) * STEP_ROWS)
+                nc.vector.quantize_mx(
+                    out=down_codes[:, cols].bitcast(FP8X4),
+                    scales=down_scales[:, cols],
+                    in_=down_grouped[:],
+                )
+
+            for s in range(STEPS + 1):
+                if s < STEPS:
+                    w_rows, v_cols = load(s)
+                    up_grouped = lay_rows_side_by_side(w_rows)
+                    v_bank, w_banks = transpose(w_rows, v_cols)
+                if s > 0:
+                    first_matmul(s - 1, w_codes, w_scales, v_codes, v_scales)
+                    quantise_down(s - 1, down_grouped)
+                if s < STEPS:
+                    v_grouped, down_grouped = empty_banks(v_bank, w_banks)
+                    w_codes, w_scales, v_codes, v_scales = quantise_up(up_grouped, v_grouped)
+
+        h_pre = keep.tile([BATCH, HIDDEN], F32)
+        nc.vector.tensor_tensor(out=h_pre[:], in0=hidden_sum[:], in1=hb_all[:], op=ADD)
+        h_p = keep.tile([BATCH, HIDDEN], F32)
+        nc.scalar.activation(out=h_p[:], in_=h_pre[:], func=SIGMOID)
+        nc.sync.dma_start(out=out_0, in_=h_p[:])
+
+        h_sorted = keep.tile([BATCH, HIDDEN], BF16)
+        nc.vector.tensor_copy(
+            out=h_sorted[:].rearrange("b (u e q) -> b u e q", u=2, e=2),
+            in_=h_p[:].rearrange("b (u q e) -> b u e q", u=2, e=2),
+        )
+        h_bank = banks.tile([P, PACK, BATCH], BF16, tag="bank")
+        for t in range(PACK):
+            nc.tensor.transpose(h_bank[:, t, :], h_sorted[:, t * P : (t + 1) * P], ident_bf16[:])
+        h_grouped = keep.tile([P, BATCH * PACK], BF16, align_bytes=64)
+        nc.vector.tensor_copy(
+            out=h_grouped[:].rearrange("p (b t) -> p b t", t=PACK),
+            in_=h_bank[:].rearrange("p t b -> p b t"),
+        )
+        h_codes = keep.tile([P, BATCH], U32, align_bytes=64)
+        h_scales = keep.tile([P, BATCH], U8, align_bytes=64)
+        nc.vector.quantize_mx(out=h_codes[:].bitcast(FP8X4), scales=h_scales[:], in_=h_grouped[:])
+
+        with tc.tile_pool(name="results", bufs=4) as results:
+            for c in range(VISIBLE // OUT_COLS):
+                result = results.tile([BATCH, OUT_COLS], F32)
+                for n in range(OUT_COLS // BANK):
+                    cols = slice(c * OUT_COLS + n * BANK, c * OUT_COLS + (n + 1) * BANK)
+                    here = slice(n * BANK, (n + 1) * BANK)
+                    down_sum = banks.tile([BATCH, BANK], F32, tag="bank")
+                    nc.tensor.matmul_mx(
+                        out=down_sum[:],
+                        lhsT=h_codes[:].bitcast(FP8X4),
+                        lhsT_scale=h_scales[:],
+                        rhs=down_codes[:, cols].bitcast(FP8X4),
+                        rhs_scale=down_scales[:, cols],
+                        start=True,
+                        stop=True,
+                    )
+                    nc.vector.tensor_tensor(
+                        out=result[:, here].rearrange("b (q r) -> b q r", r=PACK),
+                        in0=down_sum[:].rearrange("b (r q) -> b q r", r=PACK),
+                        in1=vb_all[:, cols].rearrange("b (q r) -> b q r", r=PACK),
+                        op=ADD,
+                    )
+                    nc.scalar.activation(out=result[:, here], in_=result[:, here], func=SIGMOID)
+                nc.sync.dma_start(
+                    out=out_1[:, c * OUT_COLS : (c + 1) * OUT_COLS], in_=result[:]
+                )

@@ -23,6 +23,7 @@ HIDDEN = 512
 PASSES = 2
 STEP_ROWS = PASSES * K_PASS
 STEPS = VISIBLE // STEP_ROWS
+LAG = 2
 VECTOR_COLS = 352
 RUN = 4
 BIAS_PARTS = 4
@@ -37,11 +38,16 @@ def tile_rbm_pa_k_kernel(tc, v, w, vb, hb, out_0, out_1):
     vb_rows = vb.partition_broadcast(P)
     hb_rows = hb.partition_broadcast(P)
 
-    with ExitStack() as whole:
-        whole.enter_context(tc.manual_schedule())
-        keep = whole.enter_context(tc.tile_pool(name="keep", bufs=1))
-        sum_bank = whole.enter_context(tc.psum_pool(name="sum_bank", bufs=1))
-        banks = whole.enter_context(tc.psum_pool(name="banks", bufs=7))
+    with ExitStack() as pools:
+        pools.enter_context(tc.manual_schedule())
+        keep = pools.enter_context(tc.tile_pool(name="keep", bufs=1))
+        w_pool = pools.enter_context(tc.tile_pool(name="w_pool", bufs=LAG + 3))
+        v_pool = pools.enter_context(tc.tile_pool(name="v_pool", bufs=3))
+        grouped = pools.enter_context(tc.tile_pool(name="grouped", bufs=2))
+        operands = pools.enter_context(tc.tile_pool(name="operands", bufs=2))
+        results = pools.enter_context(tc.tile_pool(name="results", bufs=4))
+        sum_bank = pools.enter_context(tc.psum_pool(name="sum_bank", bufs=1))
+        banks = pools.enter_context(tc.psum_pool(name="banks", bufs=7))
 
         ident_f32 = keep.tile([P, P], F32)
         make_identity(nc, ident_f32[:])
@@ -58,135 +64,154 @@ def tile_rbm_pa_k_kernel(tc, v, w, vb, hb, out_0, out_1):
         hb_all = keep.tile([P, HIDDEN], BF16)
         hidden_sum = sum_bank.tile([BATCH, HIDDEN], F32)
 
-        with ExitStack() as up:
-            w_pool = up.enter_context(tc.tile_pool(name="w_pool", bufs=5))
-            v_pool = up.enter_context(tc.tile_pool(name="v_pool", bufs=4))
-            grouped = up.enter_context(tc.tile_pool(name="grouped", bufs=2))
-            operands = up.enter_context(tc.tile_pool(name="operands", bufs=3))
+        w_tiles = []
+        down_banks = {}
+        down_grouped = {}
 
-            def load(s):
-                w_rows = w_pool.tile([P, PASSES * PACK * HIDDEN], BF16)
-                for g in range(PASSES):
-                    here = slice(g * PACK * HIDDEN, (g + 1) * PACK * HIDDEN)
-                    nc.sync.dma_start(out=w_rows[:, here], in_=w_steps[s, :, g, :])
-                v_cols = v_pool.tile([BATCH, STEP_ROWS], BF16)
-                nc.sync.dma_start(out=v_cols[:], in_=v[:, s * STEP_ROWS : (s + 1) * STEP_ROWS])
-                if s % BIAS_PARTS == 1:
-                    part = VISIBLE // BIAS_PARTS
-                    cols = slice((s // BIAS_PARTS) * part, (s // BIAS_PARTS + 1) * part)
-                    nc.sync.dma_start(out=vb_all[:, cols], in_=vb_rows[:, cols])
-                if s == STEPS // 2:
-                    nc.sync.dma_start(out=hb_all[:], in_=hb_rows)
-                return w_rows, v_cols
+        def load(s):
+            w_rows = w_pool.tile([P, PASSES * PACK * HIDDEN], BF16)
+            for g in range(PASSES):
+                here = slice(g * PACK * HIDDEN, (g + 1) * PACK * HIDDEN)
+                nc.sync.dma_start(out=w_rows[:, here], in_=w_steps[s, :, g, :])
+            w_tiles.append(w_rows)
+            v_cols = v_pool.tile([BATCH, STEP_ROWS], BF16)
+            nc.sync.dma_start(out=v_cols[:], in_=v[:, s * STEP_ROWS : (s + 1) * STEP_ROWS])
+            if s % BIAS_PARTS == 1:
+                part = VISIBLE // BIAS_PARTS
+                cols = slice((s // BIAS_PARTS) * part, (s // BIAS_PARTS + 1) * part)
+                nc.sync.dma_start(out=vb_all[:, cols], in_=vb_rows[:, cols])
+            if s == STEPS // 2:
+                nc.sync.dma_start(out=hb_all[:], in_=hb_rows)
+            return v_cols
 
-            def lay_rows_side_by_side(w_rows):
-                up_grouped = grouped.tile([P, PASSES * HIDDEN * PACK], BF16, align_bytes=64)
-                src = w_rows[:].rearrange("p (g r c i) -> p g c r i", g=PASSES, r=PACK, i=RUN)
-                dst = up_grouped[:].rearrange("p (g c i r) -> p g c r i", g=PASSES, r=PACK, i=RUN)
-                split = VECTOR_COLS // RUN
-                for g in range(PASSES):
-                    nc.vector.tensor_copy(out=dst[:, g, :split], in_=src[:, g, :split])
-                    nc.scalar.copy(out=dst[:, g, split:], in_=src[:, g, split:])
-                return up_grouped
+        def lay_rows_side_by_side(s):
+            up_grouped = grouped.tile([P, PASSES * HIDDEN * PACK], BF16, align_bytes=64)
+            src = w_tiles[s][:].rearrange("p (g r c i) -> p g c r i", g=PASSES, r=PACK, i=RUN)
+            dst = up_grouped[:].rearrange("p (g c i r) -> p g c r i", g=PASSES, r=PACK, i=RUN)
+            split = VECTOR_COLS // RUN
+            for g in range(PASSES):
+                nc.vector.tensor_copy(out=dst[:, g, :split], in_=src[:, g, :split])
+                nc.scalar.copy(out=dst[:, g, split:], in_=src[:, g, split:])
+            return up_grouped
 
-            def transpose(w_rows, v_cols):
-                v_words = v_cols[:].bitcast(F32).rearrange("b (g q u) -> b g u q", g=PASSES, u=2)
-                v_bank = banks.tile([P, PASSES * 2, BATCH], F32, tag="bank")
-                for g in range(PASSES):
+        def transpose_v(v_cols):
+            v_words = v_cols[:].bitcast(F32).rearrange("b (g q u) -> b g u q", g=PASSES, u=2)
+            v_bank = banks.tile([P, PASSES * 2, BATCH], F32, tag="bank")
+            for g in range(PASSES):
+                for u in range(2):
+                    nc.tensor.transpose(v_bank[:, 2 * g + u, :], v_words[:, g, u, :], ident_f32[:])
+            return v_bank
+
+        def empty_v(v_bank):
+            v_grouped = grouped.tile([P, PASSES * BATCH * PACK], BF16, align_bytes=64)
+            nc.scalar.copy(
+                out=v_grouped[:].bitcast(F32).rearrange("p (g b u) -> p g b u", g=PASSES, u=2),
+                in_=v_bank[:].rearrange("p (g u) b -> p g b u", u=2),
+            )
+            return v_grouped
+
+        def quantise_up(up_grouped, v_grouped):
+            w_codes = operands.tile([P, PASSES * HIDDEN], U32, align_bytes=64)
+            w_scales = operands.tile([P, PASSES * HIDDEN], U8, align_bytes=64)
+            nc.vector.quantize_mx(
+                out=w_codes[:].bitcast(FP8X4), scales=w_scales[:], in_=up_grouped[:]
+            )
+            v_codes = operands.tile([P, PASSES * BATCH], U32, align_bytes=64)
+            v_scales = operands.tile([P, PASSES * BATCH], U8, align_bytes=64)
+            nc.vector.quantize_mx(
+                out=v_codes[:].bitcast(FP8X4), scales=v_scales[:], in_=v_grouped[:]
+            )
+            return w_codes, w_scales, v_codes, v_scales
+
+        def first_matmul(s, w_codes, w_scales, v_codes, v_scales):
+            for g in range(PASSES):
+                b_cols = slice(g * BATCH, (g + 1) * BATCH)
+                h_cols = slice(g * HIDDEN, (g + 1) * HIDDEN)
+                nc.tensor.matmul_mx(
+                    out=hidden_sum[:],
+                    lhsT=v_codes[:, b_cols].bitcast(FP8X4),
+                    lhsT_scale=v_scales[:, b_cols],
+                    rhs=w_codes[:, h_cols].bitcast(FP8X4),
+                    rhs_scale=w_scales[:, h_cols],
+                    start=(s == 0 and g == 0),
+                    stop=(s == STEPS - 1 and g == PASSES - 1),
+                )
+
+        def transpose_down(k):
+            w_words = w_tiles[k // PASSES][:].bitcast(F32).rearrange(
+                "q (g a r u i) -> q g a r u i", g=PASSES, a=2, r=2, u=2
+            )
+            down_banks[k] = []
+            for a in range(2):
+                w_bank = banks.tile([P, 4, P], F32, tag="bank")
+                for r in range(2):
                     for u in range(2):
-                        nc.tensor.transpose(v_bank[:, 2 * g + u, :], v_words[:, g, u, :], ident_f32[:])
-                w_words = w_rows[:].bitcast(F32).rearrange(
-                    "q (g a r u i) -> q g a r u i", g=PASSES, a=2, r=2, u=2
-                )
-                w_banks = []
-                for g in range(PASSES):
-                    for a in range(2):
-                        w_bank = banks.tile([P, 4, P], F32, tag="bank", name="w_bank")
-                        for r in range(2):
-                            for u in range(2):
-                                nc.tensor.transpose(
-                                    w_bank[:, 2 * r + u, :], w_words[:, g, a, r, u, :], ident_f32[:]
-                                )
-                        w_banks.append(w_bank)
-                return v_bank, w_banks
+                        nc.tensor.transpose(
+                            w_bank[:, 2 * r + u, :], w_words[:, k % PASSES, a, r, u, :], ident_f32[:]
+                        )
+                down_banks[k].append(w_bank)
 
-            def empty_banks(v_bank, w_banks):
-                v_grouped = grouped.tile([P, PASSES * BATCH * PACK], BF16, align_bytes=64)
+        def empty_down(k):
+            rows = grouped.tile([P, K_PASS * PACK], BF16, align_bytes=64, tag="down", bufs=4)
+            dst = rows[:].bitcast(F32).rearrange("p (a r q u) -> p a r q u", a=2, r=2, u=2)
+            for a in range(2):
                 nc.scalar.copy(
-                    out=v_grouped[:].bitcast(F32).rearrange("p (g b u) -> p g b u", g=PASSES, u=2),
-                    in_=v_bank[:].rearrange("p (g u) b -> p g b u", u=2),
+                    out=dst[:, a], in_=down_banks[k][a][:].rearrange("p (r u) q -> p r q u", u=2)
                 )
-                down_grouped = grouped.tile([P, STEP_ROWS * PACK], BF16, align_bytes=64)
-                dst = down_grouped[:].bitcast(F32).rearrange(
-                    "p (n r q u) -> p n r q u", n=len(w_banks), r=2, u=2
-                )
-                for n, w_bank in enumerate(w_banks):
-                    nc.scalar.copy(
-                        out=dst[:, n], in_=w_bank[:].rearrange("p (r u) q -> p r q u", u=2)
-                    )
-                return v_grouped, down_grouped
+            down_grouped[k] = rows
 
-            def quantise_up(up_grouped, v_grouped):
-                w_codes = operands.tile([P, PASSES * HIDDEN], U32, align_bytes=64)
-                w_scales = operands.tile([P, PASSES * HIDDEN], U8, align_bytes=64)
-                nc.vector.quantize_mx(
-                    out=w_codes[:].bitcast(FP8X4), scales=w_scales[:], in_=up_grouped[:]
-                )
-                v_codes = operands.tile([P, PASSES * BATCH], U32, align_bytes=64)
-                v_scales = operands.tile([P, PASSES * BATCH], U8, align_bytes=64)
-                nc.vector.quantize_mx(
-                    out=v_codes[:].bitcast(FP8X4), scales=v_scales[:], in_=v_grouped[:]
-                )
-                return w_codes, w_scales, v_codes, v_scales
+        def quantise_down(k):
+            cols = slice(k * K_PASS, (k + 1) * K_PASS)
+            nc.vector.quantize_mx(
+                out=down_codes[:, cols].bitcast(FP8X4),
+                scales=down_scales[:, cols],
+                in_=down_grouped[k][:],
+            )
 
-            def first_matmul(s, w_codes, w_scales, v_codes, v_scales):
+        for s in range(STEPS):
+            v_cols = load(s)
+            up_grouped = lay_rows_side_by_side(s)
+            v_bank = transpose_v(v_cols)
+            if s >= LAG:
                 for g in range(PASSES):
-                    b_cols = slice(g * BATCH, (g + 1) * BATCH)
-                    h_cols = slice(g * HIDDEN, (g + 1) * HIDDEN)
-                    nc.tensor.matmul_mx(
-                        out=hidden_sum[:],
-                        lhsT=v_codes[:, b_cols].bitcast(FP8X4),
-                        lhsT_scale=v_scales[:, b_cols],
-                        rhs=w_codes[:, h_cols].bitcast(FP8X4),
-                        rhs_scale=w_scales[:, h_cols],
-                        start=(s == 0 and g == 0),
-                        stop=(s == STEPS - 1 and g == PASSES - 1),
-                    )
+                    transpose_down((s - LAG) * PASSES + g)
+            if s >= 1:
+                first_matmul(s - 1, w_codes, w_scales, v_codes, v_scales)
+            if s >= LAG + 1:
+                for g in range(PASSES):
+                    quantise_down((s - LAG - 1) * PASSES + g)
+            v_grouped = empty_v(v_bank)
+            if s >= LAG:
+                for g in range(PASSES):
+                    empty_down((s - LAG) * PASSES + g)
+            w_codes, w_scales, v_codes, v_scales = quantise_up(up_grouped, v_grouped)
 
-            def quantise_down(s, down_grouped):
-                cols = slice(s * STEP_ROWS, (s + 1) * STEP_ROWS)
-                nc.vector.quantize_mx(
-                    out=down_codes[:, cols].bitcast(FP8X4),
-                    scales=down_scales[:, cols],
-                    in_=down_grouped[:],
-                )
-
-            for s in range(STEPS + 1):
-                if s < STEPS:
-                    w_rows, v_cols = load(s)
-                    up_grouped = lay_rows_side_by_side(w_rows)
-                    v_bank, w_banks = transpose(w_rows, v_cols)
-                if s > 0:
-                    first_matmul(s - 1, w_codes, w_scales, v_codes, v_scales)
-                    quantise_down(s - 1, down_grouped)
-                if s < STEPS:
-                    v_grouped, down_grouped = empty_banks(v_bank, w_banks)
-                    w_codes, w_scales, v_codes, v_scales = quantise_up(up_grouped, v_grouped)
+        k = (STEPS - LAG - 1) * PASSES
+        transpose_down(k + 2)
+        transpose_down(k + 3)
+        first_matmul(STEPS - 1, w_codes, w_scales, v_codes, v_scales)
+        empty_down(k + 2)
+        quantise_down(k)
 
         h_pre = keep.tile([BATCH, HIDDEN], F32)
         nc.vector.tensor_tensor(out=h_pre[:], in0=hidden_sum[:], in1=hb_all[:], op=ADD)
         h_p = keep.tile([BATCH, HIDDEN], F32)
         nc.scalar.activation(out=h_p[:], in_=h_pre[:], func=SIGMOID)
         nc.sync.dma_start(out=out_0, in_=h_p[:])
+        transpose_down(k + 4)
+        transpose_down(k + 5)
+        quantise_down(k + 1)
 
         h_sorted = keep.tile([BATCH, HIDDEN], BF16)
         nc.vector.tensor_copy(
             out=h_sorted[:].rearrange("b (u e q) -> b u e q", u=2, e=2),
             in_=h_p[:].rearrange("b (u q e) -> b u e q", u=2, e=2),
         )
+        empty_down(k + 3)
         h_bank = banks.tile([P, PACK, BATCH], BF16, tag="bank")
         for t in range(PACK):
             nc.tensor.transpose(h_bank[:, t, :], h_sorted[:, t * P : (t + 1) * P], ident_bf16[:])
+        quantise_down(k + 2)
         h_grouped = keep.tile([P, BATCH * PACK], BF16, align_bytes=64)
         nc.vector.tensor_copy(
             out=h_grouped[:].rearrange("p (b t) -> p b t", t=PACK),
@@ -195,30 +220,32 @@ def tile_rbm_pa_k_kernel(tc, v, w, vb, hb, out_0, out_1):
         h_codes = keep.tile([P, BATCH], U32, align_bytes=64)
         h_scales = keep.tile([P, BATCH], U8, align_bytes=64)
         nc.vector.quantize_mx(out=h_codes[:].bitcast(FP8X4), scales=h_scales[:], in_=h_grouped[:])
+        quantise_down(k + 3)
+        empty_down(k + 4)
+        empty_down(k + 5)
 
-        with tc.tile_pool(name="results", bufs=4) as results:
-            for c in range(VISIBLE // OUT_COLS):
-                result = results.tile([BATCH, OUT_COLS], F32)
-                for n in range(OUT_COLS // BANK):
-                    cols = slice(c * OUT_COLS + n * BANK, c * OUT_COLS + (n + 1) * BANK)
-                    here = slice(n * BANK, (n + 1) * BANK)
-                    down_sum = banks.tile([BATCH, BANK], F32, tag="bank")
-                    nc.tensor.matmul_mx(
-                        out=down_sum[:],
-                        lhsT=h_codes[:].bitcast(FP8X4),
-                        lhsT_scale=h_scales[:],
-                        rhs=down_codes[:, cols].bitcast(FP8X4),
-                        rhs_scale=down_scales[:, cols],
-                        start=True,
-                        stop=True,
-                    )
-                    nc.vector.tensor_tensor(
-                        out=result[:, here].rearrange("b (q r) -> b q r", r=PACK),
-                        in0=down_sum[:].rearrange("b (r q) -> b q r", r=PACK),
-                        in1=vb_all[:, cols].rearrange("b (q r) -> b q r", r=PACK),
-                        op=ADD,
-                    )
-                    nc.scalar.activation(out=result[:, here], in_=result[:, here], func=SIGMOID)
-                nc.sync.dma_start(
-                    out=out_1[:, c * OUT_COLS : (c + 1) * OUT_COLS], in_=result[:]
+        for c in range(VISIBLE // OUT_COLS):
+            result = results.tile([BATCH, OUT_COLS], F32)
+            for n in range(OUT_COLS // BANK):
+                cols = slice(c * OUT_COLS + n * BANK, c * OUT_COLS + (n + 1) * BANK)
+                here = slice(n * BANK, (n + 1) * BANK)
+                down_sum = banks.tile([BATCH, BANK], F32, tag="bank")
+                nc.tensor.matmul_mx(
+                    out=down_sum[:],
+                    lhsT=h_codes[:].bitcast(FP8X4),
+                    lhsT_scale=h_scales[:],
+                    rhs=down_codes[:, cols].bitcast(FP8X4),
+                    rhs_scale=down_scales[:, cols],
+                    start=True,
+                    stop=True,
                 )
+                nc.vector.tensor_tensor(
+                    out=result[:, here].rearrange("b (q r) -> b q r", r=PACK),
+                    in0=down_sum[:].rearrange("b (r q) -> b q r", r=PACK),
+                    in1=vb_all[:, cols].rearrange("b (q r) -> b q r", r=PACK),
+                    op=ADD,
+                )
+                nc.scalar.activation(out=result[:, here], in_=result[:, here], func=SIGMOID)
+            nc.sync.dma_start(out=out_1[:, c * OUT_COLS : (c + 1) * OUT_COLS], in_=result[:])
+            if c < 2:
+                quantise_down(k + 4 + c)

@@ -41,11 +41,8 @@ def tile_rbm_pa_k_kernel(tc, v, w, vb, hb, out_0, out_1):
     with ExitStack() as pools:
         pools.enter_context(tc.manual_schedule())
         keep = pools.enter_context(tc.tile_pool(name="keep", bufs=1))
-        w_pool = pools.enter_context(tc.tile_pool(name="w_pool", bufs=LAG + 3))
-        v_pool = pools.enter_context(tc.tile_pool(name="v_pool", bufs=3))
-        grouped = pools.enter_context(tc.tile_pool(name="grouped", bufs=2))
-        operands = pools.enter_context(tc.tile_pool(name="operands", bufs=2))
-        results = pools.enter_context(tc.tile_pool(name="results", bufs=4))
+        w_pool = pools.enter_context(tc.tile_pool(name="w_pool", bufs=LAG + 4))
+        down_pool = pools.enter_context(tc.tile_pool(name="down_pool", bufs=2 * PASSES))
         sum_bank = pools.enter_context(tc.psum_pool(name="sum_bank", bufs=1))
         banks = pools.enter_context(tc.psum_pool(name="banks", bufs=7))
 
@@ -76,7 +73,7 @@ def tile_rbm_pa_k_kernel(tc, v, w, vb, hb, out_0, out_1):
             w_tiles.append(w_rows)
             v_cols = v_pool.tile([BATCH, STEP_ROWS], BF16)
             nc.sync.dma_start(out=v_cols[:], in_=v[:, s * STEP_ROWS : (s + 1) * STEP_ROWS])
-            if s % BIAS_PARTS == 1:
+            if s % BIAS_PARTS == BIAS_PARTS - 1:
                 part = VISIBLE // BIAS_PARTS
                 cols = slice((s // BIAS_PARTS) * part, (s // BIAS_PARTS + 1) * part)
                 nc.sync.dma_start(out=vb_all[:, cols], in_=vb_rows[:, cols])
@@ -152,7 +149,7 @@ def tile_rbm_pa_k_kernel(tc, v, w, vb, hb, out_0, out_1):
                 down_banks[k].append(w_bank)
 
         def empty_down(k):
-            rows = grouped.tile([P, K_PASS * PACK], BF16, align_bytes=64, tag="down", bufs=4)
+            rows = down_pool.tile([P, K_PASS * PACK], BF16, align_bytes=64)
             dst = rows[:].bitcast(F32).rearrange("p (a r q u) -> p a r q u", a=2, r=2, u=2)
             for a in range(2):
                 nc.scalar.copy(
@@ -168,29 +165,34 @@ def tile_rbm_pa_k_kernel(tc, v, w, vb, hb, out_0, out_1):
                 in_=down_grouped[k][:],
             )
 
-        for s in range(STEPS):
-            v_cols = load(s)
-            up_grouped = lay_rows_side_by_side(s)
-            v_bank = transpose_v(v_cols)
-            if s >= LAG:
-                for g in range(PASSES):
-                    transpose_down((s - LAG) * PASSES + g)
-            if s >= 1:
-                first_matmul(s - 1, w_codes, w_scales, v_codes, v_scales)
-            if s >= LAG + 1:
-                for g in range(PASSES):
-                    quantise_down((s - LAG - 1) * PASSES + g)
-            v_grouped = empty_v(v_bank)
-            if s >= LAG:
-                for g in range(PASSES):
-                    empty_down((s - LAG) * PASSES + g)
-            w_codes, w_scales, v_codes, v_scales = quantise_up(up_grouped, v_grouped)
+        with ExitStack() as up_pools:
+            v_pool = up_pools.enter_context(tc.tile_pool(name="v_pool", bufs=3))
+            grouped = up_pools.enter_context(tc.tile_pool(name="grouped", bufs=2))
+            operands = up_pools.enter_context(tc.tile_pool(name="operands", bufs=3))
 
-        k = (STEPS - LAG - 1) * PASSES
-        transpose_down(k + 2)
-        transpose_down(k + 3)
-        first_matmul(STEPS - 1, w_codes, w_scales, v_codes, v_scales)
-        empty_down(k + 2)
+            for s in range(STEPS):
+                v_cols = load(s)
+                up_grouped = lay_rows_side_by_side(s)
+                v_bank = transpose_v(v_cols)
+                if s >= LAG:
+                    for g in range(PASSES):
+                        transpose_down((s - LAG) * PASSES + g)
+                if s >= 1:
+                    first_matmul(s - 1, w_codes, w_scales, v_codes, v_scales)
+                if s >= LAG + 1:
+                    for g in range(PASSES):
+                        quantise_down((s - LAG - 1) * PASSES + g)
+                v_grouped = empty_v(v_bank)
+                if s >= LAG:
+                    for g in range(PASSES):
+                        empty_down((s - LAG) * PASSES + g)
+                w_codes, w_scales, v_codes, v_scales = quantise_up(up_grouped, v_grouped)
+
+            k = (STEPS - LAG - 1) * PASSES
+            transpose_down(k + 2)
+            transpose_down(k + 3)
+            first_matmul(STEPS - 1, w_codes, w_scales, v_codes, v_scales)
+        results = pools.enter_context(tc.tile_pool(name="results", bufs=8))
         quantise_down(k)
 
         h_pre = keep.tile([BATCH, HIDDEN], F32)
@@ -198,8 +200,8 @@ def tile_rbm_pa_k_kernel(tc, v, w, vb, hb, out_0, out_1):
         h_p = keep.tile([BATCH, HIDDEN], F32)
         nc.scalar.activation(out=h_p[:], in_=h_pre[:], func=SIGMOID)
         nc.sync.dma_start(out=out_0, in_=h_p[:])
+        empty_down(k + 2)
         transpose_down(k + 4)
-        transpose_down(k + 5)
         quantise_down(k + 1)
 
         h_sorted = keep.tile([BATCH, HIDDEN], BF16)
@@ -211,6 +213,7 @@ def tile_rbm_pa_k_kernel(tc, v, w, vb, hb, out_0, out_1):
         h_bank = banks.tile([P, PACK, BATCH], BF16, tag="bank")
         for t in range(PACK):
             nc.tensor.transpose(h_bank[:, t, :], h_sorted[:, t * P : (t + 1) * P], ident_bf16[:])
+        transpose_down(k + 5)
         quantise_down(k + 2)
         h_grouped = keep.tile([P, BATCH * PACK], BF16, align_bytes=64)
         nc.vector.tensor_copy(

@@ -23,8 +23,8 @@ HIDDEN = 512
 PASSES = 2
 STEP_ROWS = PASSES * K_PASS
 STEPS = VISIBLE // STEP_ROWS
-LAG = 2
-VECTOR_COLS = 352
+LAG = 3
+VECTOR_COLS = 344
 RUN = 4
 BIAS_PARTS = 4
 OUT_COLS = 1024
@@ -73,12 +73,12 @@ def tile_rbm_pa_k_kernel(tc, v, w, vb, hb, out_0, out_1):
             w_tiles.append(w_rows)
             v_cols = v_pool.tile([BATCH, STEP_ROWS], BF16)
             nc.sync.dma_start(out=v_cols[:], in_=v[:, s * STEP_ROWS : (s + 1) * STEP_ROWS])
-            if s % BIAS_PARTS == BIAS_PARTS - 1:
-                part = VISIBLE // BIAS_PARTS
-                cols = slice((s // BIAS_PARTS) * part, (s // BIAS_PARTS + 1) * part)
-                nc.sync.dma_start(out=vb_all[:, cols], in_=vb_rows[:, cols])
-            if s == STEPS // 2:
+            if s == STEPS - 1:
                 nc.sync.dma_start(out=hb_all[:], in_=hb_rows)
+                part = VISIBLE // BIAS_PARTS
+                for i in range(BIAS_PARTS):
+                    cols = slice(i * part, (i + 1) * part)
+                    nc.sync.dma_start(out=vb_all[:, cols], in_=vb_rows[:, cols])
             return v_cols
 
         def lay_rows_side_by_side(s):
@@ -191,30 +191,35 @@ def tile_rbm_pa_k_kernel(tc, v, w, vb, hb, out_0, out_1):
             k = (STEPS - LAG - 1) * PASSES
             transpose_down(k + 2)
             transpose_down(k + 3)
+            transpose_down(k + 4)
             first_matmul(STEPS - 1, w_codes, w_scales, v_codes, v_scales)
         results = pools.enter_context(tc.tile_pool(name="results", bufs=8))
         quantise_down(k)
+        empty_down(k + 2)
+        quantise_down(k + 1)
+        empty_down(k + 3)
+        transpose_down(k + 5)
 
         h_pre = keep.tile([BATCH, HIDDEN], F32)
         nc.vector.tensor_tensor(out=h_pre[:], in0=hidden_sum[:], in1=hb_all[:], op=ADD)
         h_p = keep.tile([BATCH, HIDDEN], F32)
         nc.scalar.activation(out=h_p[:], in_=h_pre[:], func=SIGMOID)
         nc.sync.dma_start(out=out_0, in_=h_p[:])
-        empty_down(k + 2)
-        transpose_down(k + 4)
-        quantise_down(k + 1)
+        empty_down(k + 4)
+        quantise_down(k + 2)
 
         h_sorted = keep.tile([BATCH, HIDDEN], BF16)
         nc.vector.tensor_copy(
             out=h_sorted[:].rearrange("b (u e q) -> b u e q", u=2, e=2),
             in_=h_p[:].rearrange("b (u q e) -> b u e q", u=2, e=2),
         )
-        empty_down(k + 3)
+        empty_down(k + 5)
         h_bank = banks.tile([P, PACK, BATCH], BF16, tag="bank")
         for t in range(PACK):
             nc.tensor.transpose(h_bank[:, t, :], h_sorted[:, t * P : (t + 1) * P], ident_bf16[:])
-        transpose_down(k + 5)
-        quantise_down(k + 2)
+        transpose_down(k + 6)
+        transpose_down(k + 7)
+        quantise_down(k + 3)
         h_grouped = keep.tile([P, BATCH * PACK], BF16, align_bytes=64)
         nc.vector.tensor_copy(
             out=h_grouped[:].rearrange("p (b t) -> p b t", t=PACK),
@@ -223,9 +228,10 @@ def tile_rbm_pa_k_kernel(tc, v, w, vb, hb, out_0, out_1):
         h_codes = keep.tile([P, BATCH], U32, align_bytes=64)
         h_scales = keep.tile([P, BATCH], U8, align_bytes=64)
         nc.vector.quantize_mx(out=h_codes[:].bitcast(FP8X4), scales=h_scales[:], in_=h_grouped[:])
-        quantise_down(k + 3)
-        empty_down(k + 4)
-        empty_down(k + 5)
+        quantise_down(k + 4)
+        quantise_down(k + 5)
+        empty_down(k + 6)
+        empty_down(k + 7)
 
         for c in range(VISIBLE // OUT_COLS):
             result = results.tile([BATCH, OUT_COLS], F32)
@@ -251,4 +257,4 @@ def tile_rbm_pa_k_kernel(tc, v, w, vb, hb, out_0, out_1):
                 nc.scalar.activation(out=result[:, here], in_=result[:, here], func=SIGMOID)
             nc.sync.dma_start(out=out_1[:, c * OUT_COLS : (c + 1) * OUT_COLS], in_=result[:])
             if c < 2:
-                quantise_down(k + 4 + c)
+                quantise_down(k + 6 + c)

@@ -25,6 +25,8 @@ STEP_ROWS = PASSES * K_PASS
 STEPS = VISIBLE // STEP_ROWS
 LAG = 3
 VECTOR_COLS = 344
+TENSOR_COLS = 96
+SCALAR_END = HIDDEN - TENSOR_COLS
 RUN = 4
 BIAS_PARTS = 4
 OUT_COLS = 1024
@@ -88,8 +90,27 @@ def tile_rbm_pa_k_kernel(tc, v, w, vb, hb, out_0, out_1):
             split = VECTOR_COLS // RUN
             for g in range(PASSES):
                 nc.vector.tensor_copy(out=dst[:, g, :split], in_=src[:, g, :split])
-                nc.scalar.copy(out=dst[:, g, split:], in_=src[:, g, split:])
+                nc.scalar.copy(out=dst[:, g, split : SCALAR_END // RUN], in_=src[:, g, split : SCALAR_END // RUN])
             return up_grouped
+
+        def spread_rows(s):
+            rows = w_tiles[s][:].rearrange("p (g r c) -> p g c r", g=PASSES, r=PACK)
+            spread = banks.tile([P, PASSES, TENSOR_COLS, PACK], BF16, tag="bank")
+            for g in range(PASSES):
+                nc.tensor.matmul(
+                    out=spread[:, g],
+                    lhsT=ident_bf16[:],
+                    rhs=rows[:, g, SCALAR_END:, :],
+                    start=True,
+                    stop=True,
+                )
+            return spread
+
+        def empty_spread(spread, up_grouped):
+            nc.scalar.copy(
+                out=up_grouped[:].rearrange("p (g c r) -> p g c r", g=PASSES, r=PACK)[:, :, SCALAR_END:, :],
+                in_=spread[:],
+            )
 
         def transpose_v(v_cols):
             v_words = v_cols[:].bitcast(F32).rearrange("b (g q u) -> b g u q", g=PASSES, u=2)
@@ -174,6 +195,7 @@ def tile_rbm_pa_k_kernel(tc, v, w, vb, hb, out_0, out_1):
                 v_cols = load(s)
                 up_grouped = lay_rows_side_by_side(s)
                 v_bank = transpose_v(v_cols)
+                spread = spread_rows(s)
                 if s >= LAG:
                     for g in range(PASSES):
                         transpose_down((s - LAG) * PASSES + g)
@@ -183,6 +205,7 @@ def tile_rbm_pa_k_kernel(tc, v, w, vb, hb, out_0, out_1):
                     for g in range(PASSES):
                         quantise_down((s - LAG - 1) * PASSES + g)
                 v_grouped = empty_v(v_bank)
+                empty_spread(spread, up_grouped)
                 if s >= LAG:
                     for g in range(PASSES):
                         empty_down((s - LAG) * PASSES + g)

@@ -24,7 +24,7 @@ PASSES = 2
 STEP_ROWS = PASSES * K_PASS
 STEPS = VISIBLE // STEP_ROWS
 LAG = 3
-VECTOR_COLS = 344
+VECTOR_COLS = 320
 TENSOR_COLS = 96
 SCALAR_END = HIDDEN - TENSOR_COLS
 RUN = 4
@@ -194,8 +194,8 @@ def tile_rbm_pa_k_kernel(tc, v, w, vb, hb, out_0, out_1):
             for s in range(STEPS):
                 v_cols = load(s)
                 up_grouped = lay_rows_side_by_side(s)
-                v_bank = transpose_v(v_cols)
                 spread = spread_rows(s)
+                v_bank = transpose_v(v_cols)
                 if s >= LAG:
                     for g in range(PASSES):
                         transpose_down((s - LAG) * PASSES + g)
@@ -204,8 +204,8 @@ def tile_rbm_pa_k_kernel(tc, v, w, vb, hb, out_0, out_1):
                 if s >= LAG + 1:
                     for g in range(PASSES):
                         quantise_down((s - LAG - 1) * PASSES + g)
-                v_grouped = empty_v(v_bank)
                 empty_spread(spread, up_grouped)
+                v_grouped = empty_v(v_bank)
                 if s >= LAG:
                     for g in range(PASSES):
                         empty_down((s - LAG) * PASSES + g)

@@ -24,7 +24,8 @@ PASSES = 2
 STEP_ROWS = PASSES * K_PASS
 STEPS = VISIBLE // STEP_ROWS
 LAG = 3
-VECTOR_COLS = 320
+DOWN_IN_LOOP = (STEPS - LAG) * PASSES
+VECTOR_COLS = 304
 TENSOR_COLS = 96
 SCALAR_END = HIDDEN - TENSOR_COLS
 RUN = 4
@@ -66,6 +67,9 @@ def tile_rbm_pa_k_kernel(tc, v, w, vb, hb, out_0, out_1):
         w_tiles = []
         down_banks = {}
         down_grouped = {}
+
+        def down_due(s):
+            return DOWN_IN_LOOP * max(s, 0) // (STEPS - 1)
 
         def load(s):
             w_rows = w_pool.tile([P, PASSES * PACK * HIDDEN], BF16)
@@ -196,19 +200,16 @@ def tile_rbm_pa_k_kernel(tc, v, w, vb, hb, out_0, out_1):
                 up_grouped = lay_rows_side_by_side(s)
                 spread = spread_rows(s)
                 v_bank = transpose_v(v_cols)
-                if s >= LAG:
-                    for g in range(PASSES):
-                        transpose_down((s - LAG) * PASSES + g)
+                for k in range(down_due(s - 1), down_due(s)):
+                    transpose_down(k)
                 if s >= 1:
                     first_matmul(s - 1, w_codes, w_scales, v_codes, v_scales)
-                if s >= LAG + 1:
-                    for g in range(PASSES):
-                        quantise_down((s - LAG - 1) * PASSES + g)
+                for k in range(down_due(s - 2), down_due(s - 1)):
+                    quantise_down(k)
                 empty_spread(spread, up_grouped)
                 v_grouped = empty_v(v_bank)
-                if s >= LAG:
-                    for g in range(PASSES):
-                        empty_down((s - LAG) * PASSES + g)
+                for k in range(down_due(s - 1), down_due(s)):
+                    empty_down(k)
                 w_codes, w_scales, v_codes, v_scales = quantise_up(up_grouped, v_grouped)
 
             k = (STEPS - LAG - 1) * PASSES

@@ -25,12 +25,13 @@ STEP_ROWS = PASSES * K_PASS
 STEPS = VISIBLE // STEP_ROWS
 LAG = 3
 DOWN_IN_LOOP = (STEPS - LAG) * PASSES
-VECTOR_COLS = 304
+VECTOR_COLS = 288
 TENSOR_COLS = 96
 SCALAR_END = HIDDEN - TENSOR_COLS
 RUN = 4
 BIAS_PARTS = 4
 OUT_COLS = 1024
+STORE_COLS = (VISIBLE // OUT_COLS - 1) * [OUT_COLS] + 2 * [BANK]
 
 FLOPS = 2 * 2 * BATCH * VISIBLE * HIDDEN
 
@@ -69,7 +70,7 @@ def tile_rbm_pa_k_kernel(tc, v, w, vb, hb, out_0, out_1):
         down_grouped = {}
 
         def down_due(s):
-            return DOWN_IN_LOOP * max(s, 0) // (STEPS - 1)
+            return DOWN_IN_LOOP * max(s + 1, 0) // STEPS
 
         def load(s):
             w_rows = w_pool.tile([P, PASSES * PACK * HIDDEN], BF16)
@@ -87,22 +88,20 @@ def tile_rbm_pa_k_kernel(tc, v, w, vb, hb, out_0, out_1):
                     nc.sync.dma_start(out=vb_all[:, cols], in_=vb_rows[:, cols])
             return v_cols
 
-        def lay_rows_side_by_side(s):
-            up_grouped = grouped.tile([P, PASSES * HIDDEN * PACK], BF16, align_bytes=64)
+        def lay_rows_side_by_side(s, up_grouped, passes):
             src = w_tiles[s][:].rearrange("p (g r c i) -> p g c r i", g=PASSES, r=PACK, i=RUN)
             dst = up_grouped[:].rearrange("p (g c i r) -> p g c r i", g=PASSES, r=PACK, i=RUN)
             split = VECTOR_COLS // RUN
-            for g in range(PASSES):
+            for g in passes:
                 nc.vector.tensor_copy(out=dst[:, g, :split], in_=src[:, g, :split])
                 nc.scalar.copy(out=dst[:, g, split : SCALAR_END // RUN], in_=src[:, g, split : SCALAR_END // RUN])
-            return up_grouped
 
-        def spread_rows(s):
+        def spread_rows(s, passes):
             rows = w_tiles[s][:].rearrange("p (g r c) -> p g c r", g=PASSES, r=PACK)
-            spread = banks.tile([P, PASSES, TENSOR_COLS, PACK], BF16, tag="bank")
-            for g in range(PASSES):
+            spread = banks.tile([P, len(passes), TENSOR_COLS, PACK], BF16, tag="bank")
+            for i, g in enumerate(passes):
                 nc.tensor.matmul(
-                    out=spread[:, g],
+                    out=spread[:, i],
                     lhsT=ident_bf16[:],
                     rhs=rows[:, g, SCALAR_END:, :],
                     start=True,
@@ -110,10 +109,10 @@ def tile_rbm_pa_k_kernel(tc, v, w, vb, hb, out_0, out_1):
                 )
             return spread
 
-        def empty_spread(spread, up_grouped):
+        def empty_spread(spread, up_grouped, passes):
+            dst = up_grouped[:].rearrange("p (g c r) -> p g c r", g=PASSES, r=PACK)
             nc.scalar.copy(
-                out=up_grouped[:].rearrange("p (g c r) -> p g c r", g=PASSES, r=PACK)[:, :, SCALAR_END:, :],
-                in_=spread[:],
+                out=dst[:, passes.start : passes.stop, SCALAR_END:, :], in_=spread[:]
             )
 
         def transpose_v(v_cols):
@@ -132,18 +131,21 @@ def tile_rbm_pa_k_kernel(tc, v, w, vb, hb, out_0, out_1):
             )
             return v_grouped
 
-        def quantise_up(up_grouped, v_grouped):
-            w_codes = operands.tile([P, PASSES * HIDDEN], U32, align_bytes=64)
-            w_scales = operands.tile([P, PASSES * HIDDEN], U8, align_bytes=64)
+        def quantise_w(up_grouped, w_codes, w_scales, passes):
+            cols = slice(passes.start * HIDDEN, passes.stop * HIDDEN)
             nc.vector.quantize_mx(
-                out=w_codes[:].bitcast(FP8X4), scales=w_scales[:], in_=up_grouped[:]
+                out=w_codes[:, cols].bitcast(FP8X4),
+                scales=w_scales[:, cols],
+                in_=up_grouped[:, passes.start * HIDDEN * PACK : passes.stop * HIDDEN * PACK],
             )
+
+        def quantise_v(v_grouped):
             v_codes = operands.tile([P, PASSES * BATCH], U32, align_bytes=64)
             v_scales = operands.tile([P, PASSES * BATCH], U8, align_bytes=64)
             nc.vector.quantize_mx(
                 out=v_codes[:].bitcast(FP8X4), scales=v_scales[:], in_=v_grouped[:]
             )
-            return w_codes, w_scales, v_codes, v_scales
+            return v_codes, v_scales
 
         def first_matmul(s, w_codes, w_scales, v_codes, v_scales):
             for g in range(PASSES):
@@ -197,20 +199,39 @@ def tile_rbm_pa_k_kernel(tc, v, w, vb, hb, out_0, out_1):
 
             for s in range(STEPS):
                 v_cols = load(s)
-                up_grouped = lay_rows_side_by_side(s)
-                spread = spread_rows(s)
-                v_bank = transpose_v(v_cols)
+                up_grouped = grouped.tile([P, PASSES * HIDDEN * PACK], BF16, align_bytes=64)
+                both = range(PASSES)
+                if s == 0:
+                    w_codes = operands.tile([P, PASSES * HIDDEN], U32, align_bytes=64)
+                    w_scales = operands.tile([P, PASSES * HIDDEN], U8, align_bytes=64)
+                    for g in both:
+                        one = range(g, g + 1)
+                        lay_rows_side_by_side(s, up_grouped, one)
+                        empty_spread(spread_rows(s, one), up_grouped, one)
+                        quantise_w(up_grouped, w_codes, w_scales, one)
+                    v_bank = transpose_v(v_cols)
+                else:
+                    lay_rows_side_by_side(s, up_grouped, both)
+                    if s == 1:
+                        v_codes, v_scales = quantise_v(v_grouped)
+                    spread = spread_rows(s, both)
+                    v_bank = transpose_v(v_cols)
                 for k in range(down_due(s - 1), down_due(s)):
                     transpose_down(k)
                 if s >= 1:
                     first_matmul(s - 1, w_codes, w_scales, v_codes, v_scales)
                 for k in range(down_due(s - 2), down_due(s - 1)):
                     quantise_down(k)
-                empty_spread(spread, up_grouped)
+                if s >= 1:
+                    empty_spread(spread, up_grouped, both)
                 v_grouped = empty_v(v_bank)
                 for k in range(down_due(s - 1), down_due(s)):
                     empty_down(k)
-                w_codes, w_scales, v_codes, v_scales = quantise_up(up_grouped, v_grouped)
+                if s >= 1:
+                    w_codes = operands.tile([P, PASSES * HIDDEN], U32, align_bytes=64)
+                    w_scales = operands.tile([P, PASSES * HIDDEN], U8, align_bytes=64)
+                    quantise_w(up_grouped, w_codes, w_scales, both)
+                    v_codes, v_scales = quantise_v(v_grouped)
 
             k = (STEPS - LAG - 1) * PASSES
             transpose_down(k + 2)
@@ -257,10 +278,11 @@ def tile_rbm_pa_k_kernel(tc, v, w, vb, hb, out_0, out_1):
         empty_down(k + 6)
         empty_down(k + 7)
 
-        for c in range(VISIBLE // OUT_COLS):
+        first = 0
+        for c, width in enumerate(STORE_COLS):
             result = results.tile([BATCH, OUT_COLS], F32)
-            for n in range(OUT_COLS // BANK):
-                cols = slice(c * OUT_COLS + n * BANK, c * OUT_COLS + (n + 1) * BANK)
+            for n in range(width // BANK):
+                cols = slice(first + n * BANK, first + (n + 1) * BANK)
                 here = slice(n * BANK, (n + 1) * BANK)
                 down_sum = banks.tile([BATCH, BANK], F32, tag="bank")
                 nc.tensor.matmul_mx(
@@ -279,6 +301,7 @@ def tile_rbm_pa_k_kernel(tc, v, w, vb, hb, out_0, out_1):
                     op=ADD,
                 )
                 nc.scalar.activation(out=result[:, here], in_=result[:, here], func=SIGMOID)
-            nc.sync.dma_start(out=out_1[:, c * OUT_COLS : (c + 1) * OUT_COLS], in_=result[:])
+            nc.sync.dma_start(out=out_1[:, first : first + width], in_=result[:, :width])
+            first += width
             if c < 2:
                 quantise_down(k + 6 + c)

@@ -25,10 +25,10 @@ STEP_ROWS = PASSES * K_PASS
 STEPS = VISIBLE // STEP_ROWS
 LAG = 3
 DOWN_IN_LOOP = (STEPS - LAG) * PASSES
-VECTOR_COLS = 288
+VECTOR_COLS = 304
 TENSOR_COLS = 96
 SCALAR_END = HIDDEN - TENSOR_COLS
-RUN = 4
+RUN = 8
 BIAS_PARTS = 4
 OUT_COLS = 1024
 STORE_COLS = (VISIBLE // OUT_COLS - 1) * [OUT_COLS] + 2 * [BANK]
@@ -92,9 +92,10 @@ def tile_rbm_pa_k_kernel(tc, v, w, vb, hb, out_0, out_1):
             src = w_tiles[s][:].rearrange("p (g r c i) -> p g c r i", g=PASSES, r=PACK, i=RUN)
             dst = up_grouped[:].rearrange("p (g c i r) -> p g c r i", g=PASSES, r=PACK, i=RUN)
             split = VECTOR_COLS // RUN
-            for g in passes:
-                nc.vector.tensor_copy(out=dst[:, g, :split], in_=src[:, g, :split])
-                nc.scalar.copy(out=dst[:, g, split : SCALAR_END // RUN], in_=src[:, g, split : SCALAR_END // RUN])
+            gs = slice(passes.start, passes.stop)
+            end = SCALAR_END // RUN
+            nc.vector.tensor_copy(out=dst[:, gs, :split], in_=src[:, gs, :split])
+            nc.scalar.copy(out=dst[:, gs, split:end], in_=src[:, gs, split:end])
 
         def spread_rows(s, passes):
             rows = w_tiles[s][:].rearrange("p (g r c) -> p g c r", g=PASSES, r=PACK)

@@ -92,10 +92,10 @@ def tile_rbm_pa_k_kernel(tc, v, w, vb, hb, out_0, out_1):
             src = w_tiles[s][:].rearrange("p (g r c i) -> p g c r i", g=PASSES, r=PACK, i=RUN)
             dst = up_grouped[:].rearrange("p (g c i r) -> p g c r i", g=PASSES, r=PACK, i=RUN)
             split = VECTOR_COLS // RUN
-            gs = slice(passes.start, passes.stop)
             end = SCALAR_END // RUN
-            nc.vector.tensor_copy(out=dst[:, gs, :split], in_=src[:, gs, :split])
-            nc.scalar.copy(out=dst[:, gs, split:end], in_=src[:, gs, split:end])
+            for g in passes:
+                nc.vector.tensor_copy(out=dst[:, g, :split], in_=src[:, g, :split])
+                nc.scalar.copy(out=dst[:, g, split:end], in_=src[:, g, split:end])
 
         def spread_rows(s, passes):
             rows = w_tiles[s][:].rearrange("p (g r c) -> p g c r", g=PASSES, r=PACK)
@@ -112,9 +112,8 @@ def tile_rbm_pa_k_kernel(tc, v, w, vb, hb, out_0, out_1):
 
         def empty_spread(spread, up_grouped, passes):
             dst = up_grouped[:].rearrange("p (g c r) -> p g c r", g=PASSES, r=PACK)
-            nc.scalar.copy(
-                out=dst[:, passes.start : passes.stop, SCALAR_END:, :], in_=spread[:]
-            )
+            for i, g in enumerate(passes):
+                nc.scalar.copy(out=dst[:, g, SCALAR_END:, :], in_=spread[:, i])
 
         def transpose_v(v_cols):
             v_words = v_cols[:].bitcast(F32).rearrange("b (g q u) -> b g u q", g=PASSES, u=2)

from contextlib import ExitStack

import concourse.mybir as mybir
from concourse.masks import make_identity

F32 = mybir.dt.float32
BF16 = mybir.dt.bfloat16
U32 = mybir.dt.uint32
U8 = mybir.dt.uint8
FP8X4 = mybir.dt.float8_e4m3fn_x4
ADD = mybir.AluOpType.add
SIGMOID = mybir.ActivationFunctionType.Sigmoid

P = 128
PACK = 4
K_PASS = P * PACK
BANK = 512

BATCH = 128
VISIBLE = 16384
HIDDEN = 512

PASSES = 2
STEP_ROWS = PASSES * K_PASS
STEPS = VISIBLE // STEP_ROWS
LAG = 3
DOWN_IN_LOOP = (STEPS - LAG) * PASSES
VECTOR_COLS = 304
TENSOR_COLS = 96
SCALAR_END = HIDDEN - TENSOR_COLS
RUN = 8
BIAS_PARTS = 4
OUT_COLS = 1024
STORE_COLS = (VISIBLE // OUT_COLS - 1) * [OUT_COLS] + 2 * [BANK]

FLOPS = 2 * 2 * BATCH * VISIBLE * HIDDEN


def tile_rbm_pa_k_kernel(tc, v, w, vb, hb, out_0, out_1):
    nc = tc.nc
    w_steps = w.rearrange("(s g p r) h -> s p g (r h)", g=PASSES, p=P, r=PACK)
    vb_rows = vb.partition_broadcast(P)
    hb_rows = hb.partition_broadcast(P)

    with ExitStack() as pools:
        pools.enter_context(tc.manual_schedule())
        keep = pools.enter_context(tc.tile_pool(name="keep", bufs=1))
        w_pool = pools.enter_context(tc.tile_pool(name="w_pool", bufs=LAG + 4))
        down_pool = pools.enter_context(tc.tile_pool(name="down_pool", bufs=2 * PASSES))
        sum_bank = pools.enter_context(tc.psum_pool(name="sum_bank", bufs=1))
        banks = pools.enter_context(tc.psum_pool(name="banks", bufs=7))

        ident_f32 = keep.tile([P, P], F32)
        make_identity(nc, ident_f32[:])
        ident_bf16 = keep.tile([P, P], BF16)
        make_identity(nc, ident_bf16[:])

        warm = keep.tile([P, 2], F32)
        nc.vector.memset(warm[:], 0.0)
        nc.scalar.activation(out=warm[:, 1:2], in_=warm[:, 0:1], func=SIGMOID)

        down_codes = keep.tile([P, VISIBLE], U32, align_bytes=64)
        down_scales = keep.tile([P, VISIBLE], U8, align_bytes=64)
        vb_all = keep.tile([P, VISIBLE], BF16)
        hb_all = keep.tile([P, HIDDEN], BF16)
        hidden_sum = sum_bank.tile([BATCH, HIDDEN], F32)

        w_tiles = []
        down_banks = {}
        down_grouped = {}

        def down_due(s):
            return DOWN_IN_LOOP * max(s + 1, 0) // STEPS

        def load(s):
            w_rows = w_pool.tile([P, PASSES * PACK * HIDDEN], BF16)
            for g in range(PASSES):
                here = slice(g * PACK * HIDDEN, (g + 1) * PACK * HIDDEN)
                nc.sync.dma_start(out=w_rows[:, here], in_=w_steps[s, :, g, :])
            w_tiles.append(w_rows)
            v_cols = v_pool.tile([BATCH, STEP_ROWS], BF16)
            nc.sync.dma_start(out=v_cols[:], in_=v[:, s * STEP_ROWS : (s + 1) * STEP_ROWS])
            if s == STEPS - 1:
                nc.sync.dma_start(out=hb_all[:], in_=hb_rows)
                part = VISIBLE // BIAS_PARTS
                for i in range(BIAS_PARTS):
                    cols = slice(i * part, (i + 1) * part)
                    nc.sync.dma_start(out=vb_all[:, cols], in_=vb_rows[:, cols])
            return v_cols

        def lay_rows_side_by_side(s, up_grouped, passes):
            src = w_tiles[s][:].rearrange("p (g r c i) -> p g c r i", g=PASSES, r=PACK, i=RUN)
            dst = up_grouped[:].rearrange("p (g c i r) -> p g c r i", g=PASSES, r=PACK, i=RUN)
            split = VECTOR_COLS // RUN
            end = SCALAR_END // RUN
            for g in passes:
                nc.vector.tensor_copy(out=dst[:, g, :split], in_=src[:, g, :split])
                nc.scalar.copy(out=dst[:, g, split:end], in_=src[:, g, split:end])

        def spread_rows(s, passes):
            rows = w_tiles[s][:].rearrange("p (g r c) -> p g c r", g=PASSES, r=PACK)
            spread = banks.tile([P, len(passes), TENSOR_COLS, PACK], BF16, tag="bank")
            for i, g in enumerate(passes):
                nc.tensor.matmul(
                    out=spread[:, i],
                    lhsT=ident_bf16[:],
                    rhs=rows[:, g, SCALAR_END:, :],
                    start=True,
                    stop=True,
                )
            return spread

        def empty_spread(spread, up_grouped, passes):
            dst = up_grouped[:].rearrange("p (g c r) -> p g c r", g=PASSES, r=PACK)
            for i, g in enumerate(passes):
                nc.scalar.copy(out=dst[:, g, SCALAR_END:, :], in_=spread[:, i])

        def transpose_v(v_cols):
            v_words = v_cols[:].bitcast(F32).rearrange("b (g q u) -> b g u q", g=PASSES, u=2)
            v_bank = banks.tile([P, PASSES * 2, BATCH], F32, tag="bank")
            for g in range(PASSES):
                for u in range(2):
                    nc.tensor.transpose(v_bank[:, 2 * g + u, :], v_words[:, g, u, :], ident_f32[:])
            return v_bank

        def empty_v(v_bank):
            v_grouped = grouped.tile([P, PASSES * BATCH * PACK], BF16, align_bytes=64)
            nc.scalar.copy(
                out=v_grouped[:].bitcast(F32).rearrange("p (g b u) -> p g b u", g=PASSES, u=2),
                in_=v_bank[:].rearrange("p (g u) b -> p g b u", u=2),
            )
            return v_grouped

        def quantise_w(up_grouped, w_codes, w_scales, passes):
            cols = slice(passes.start * HIDDEN, passes.stop * HIDDEN)
            nc.vector.quantize_mx(
                out=w_codes[:, cols].bitcast(FP8X4),
                scales=w_scales[:, cols],
                in_=up_grouped[:, passes.start * HIDDEN * PACK : passes.stop * HIDDEN * PACK],
            )

        def quantise_v(v_grouped):
            v_codes = operands.tile([P, PASSES * BATCH], U32, align_bytes=64)
            v_scales = operands.tile([P, PASSES * BATCH], U8, align_bytes=64)
            nc.vector.quantize_mx(
                out=v_codes[:].bitcast(FP8X4), scales=v_scales[:], in_=v_grouped[:]
            )
            return v_codes, v_scales

        def first_matmul(s, w_codes, w_scales, v_codes, v_scales):
            for g in range(PASSES):
                b_cols = slice(g * BATCH, (g + 1) * BATCH)
                h_cols = slice(g * HIDDEN, (g + 1) * HIDDEN)
                nc.tensor.matmul_mx(
                    out=hidden_sum[:],
                    lhsT=v_codes[:, b_cols].bitcast(FP8X4),
                    lhsT_scale=v_scales[:, b_cols],
                    rhs=w_codes[:, h_cols].bitcast(FP8X4),
                    rhs_scale=w_scales[:, h_cols],
                    start=(s == 0 and g == 0),
                    stop=(s == STEPS - 1 and g == PASSES - 1),
                )

        def transpose_down(k):
            w_words = w_tiles[k // PASSES][:].bitcast(F32).rearrange(
                "q (g a r u i) -> q g a r u i", g=PASSES, a=2, r=2, u=2
            )
            down_banks[k] = []
            for a in range(2):
                w_bank = banks.tile([P, 4, P], F32, tag="bank")
                for r in range(2):
                    for u in range(2):
                        nc.tensor.transpose(
                            w_bank[:, 2 * r + u, :], w_words[:, k % PASSES, a, r, u, :], ident_f32[:]
                        )
                down_banks[k].append(w_bank)

        def empty_down(k):
            rows = down_pool.tile([P, K_PASS * PACK], BF16, align_bytes=64)
            dst = rows[:].bitcast(F32).rearrange("p (a r q u) -> p a r q u", a=2, r=2, u=2)
            for a in range(2):
                nc.scalar.copy(
                    out=dst[:, a], in_=down_banks[k][a][:].rearrange("p (r u) q -> p r q u", u=2)
                )
            down_grouped[k] = rows

        def quantise_down(k):
            cols = slice(k * K_PASS, (k + 1) * K_PASS)
            nc.vector.quantize_mx(
                out=down_codes[:, cols].bitcast(FP8X4),
                scales=down_scales[:, cols],
                in_=down_grouped[k][:],
            )

        with ExitStack() as up_pools:
            v_pool = up_pools.enter_context(tc.tile_pool(name="v_pool", bufs=3))
            grouped = up_pools.enter_context(tc.tile_pool(name="grouped", bufs=2))
            operands = up_pools.enter_context(tc.tile_pool(name="operands", bufs=3))

            for s in range(STEPS):
                v_cols = load(s)
                up_grouped = grouped.tile([P, PASSES * HIDDEN * PACK], BF16, align_bytes=64)
                both = range(PASSES)
                if s == 0:
                    w_codes = operands.tile([P, PASSES * HIDDEN], U32, align_bytes=64)
                    w_scales = operands.tile([P, PASSES * HIDDEN], U8, align_bytes=64)
                    for g in both:
                        one = range(g, g + 1)
                        lay_rows_side_by_side(s, up_grouped, one)
                        empty_spread(spread_rows(s, one), up_grouped, one)
                        quantise_w(up_grouped, w_codes, w_scales, one)
                    v_bank = transpose_v(v_cols)
                else:
                    lay_rows_side_by_side(s, up_grouped, both)
                    if s == 1:
                        v_codes, v_scales = quantise_v(v_grouped)
                    spread = spread_rows(s, both)
                    v_bank = transpose_v(v_cols)
                for k in range(down_due(s - 1), down_due(s)):
                    transpose_down(k)
                if s >= 1:
                    first_matmul(s - 1, w_codes, w_scales, v_codes, v_scales)
                for k in range(down_due(s - 2), down_due(s - 1)):
                    quantise_down(k)
                if s >= 1:
                    empty_spread(spread, up_grouped, both)
                v_grouped = empty_v(v_bank)
                for k in range(down_due(s - 1), down_due(s)):
                    empty_down(k)
                if s >= 1:
                    w_codes = operands.tile([P, PASSES * HIDDEN], U32, align_bytes=64)
                    w_scales = operands.tile([P, PASSES * HIDDEN], U8, align_bytes=64)
                    quantise_w(up_grouped, w_codes, w_scales, both)
                    v_codes, v_scales = quantise_v(v_grouped)

            k = (STEPS - LAG - 1) * PASSES
            transpose_down(k + 2)
            transpose_down(k + 3)
            transpose_down(k + 4)
            first_matmul(STEPS - 1, w_codes, w_scales, v_codes, v_scales)
        results = pools.enter_context(tc.tile_pool(name="results", bufs=8))
        quantise_down(k)
        empty_down(k + 2)
        quantise_down(k + 1)
        empty_down(k + 3)
        transpose_down(k + 5)

        h_pre = keep.tile([BATCH, HIDDEN], F32)
        nc.vector.tensor_tensor(out=h_pre[:], in0=hidden_sum[:], in1=hb_all[:], op=ADD)
        h_p = keep.tile([BATCH, HIDDEN], F32)
        nc.scalar.activation(out=h_p[:], in_=h_pre[:], func=SIGMOID)
        nc.sync.dma_start(out=out_0, in_=h_p[:])
        empty_down(k + 4)
        quantise_down(k + 2)

        h_sorted = keep.tile([BATCH, HIDDEN], BF16)
        nc.vector.tensor_copy(
            out=h_sorted[:].rearrange("b (u e q) -> b u e q", u=2, e=2),
            in_=h_p[:].rearrange("b (u q e) -> b u e q", u=2, e=2),
        )
        empty_down(k + 5)
        h_bank = banks.tile([P, PACK, BATCH], BF16, tag="bank")
        for t in range(PACK):
            nc.tensor.transpose(h_bank[:, t, :], h_sorted[:, t * P : (t + 1) * P], ident_bf16[:])
        transpose_down(k + 6)
        transpose_down(k + 7)
        quantise_down(k + 3)
        h_grouped = keep.tile([P, BATCH * PACK], BF16, align_bytes=64)
        nc.vector.tensor_copy(
            out=h_grouped[:].rearrange("p (b t) -> p b t", t=PACK),
            in_=h_bank[:].rearrange("p t b -> p b t"),
        )
        h_codes = keep.tile([P, BATCH], U32, align_bytes=64)
        h_scales = keep.tile([P, BATCH], U8, align_bytes=64)
        nc.vector.quantize_mx(out=h_codes[:].bitcast(FP8X4), scales=h_scales[:], in_=h_grouped[:])
        quantise_down(k + 4)
        quantise_down(k + 5)
        empty_down(k + 6)
        empty_down(k + 7)

        first = 0
        for c, width in enumerate(STORE_COLS):
            result = results.tile([BATCH, OUT_COLS], F32)
            for n in range(width // BANK):
                cols = slice(first + n * BANK, first + (n + 1) * BANK)
                here = slice(n * BANK, (n + 1) * BANK)
                down_sum = banks.tile([BATCH, BANK], F32, tag="bank")
                nc.tensor.matmul_mx(
                    out=down_sum[:],
                    lhsT=h_codes[:].bitcast(FP8X4),
                    lhsT_scale=h_scales[:],
                    rhs=down_codes[:, cols].bitcast(FP8X4),
                    rhs_scale=down_scales[:, cols],
                    start=True,
                    stop=True,
                )
                nc.vector.tensor_tensor(
                    out=result[:, here].rearrange("b (q r) -> b q r", r=PACK),
                    in0=down_sum[:].rearrange("b (r q) -> b q r", r=PACK),
                    in1=vb_all[:, cols].rearrange("b (q r) -> b q r", r=PACK),
                    op=ADD,
                )
                nc.scalar.activation(out=result[:, here], in_=result[:, here], func=SIGMOID)
            nc.sync.dma_start(out=out_1[:, first : first + width], in_=result[:, :width])
            first += width
            if c < 2:
                quantise_down(k + 6 + c)
